import numpy as np
import ml_dtypes


def mxq(x, axis, fmt="e4m3"):
    dtype, down = {"e4m3": (ml_dtypes.float8_e4m3fn, 7), "e5m2": (ml_dtypes.float8_e5m2, 14)}[fmt]
    v = np.moveaxis(np.asarray(x, np.float32).astype(ml_dtypes.bfloat16).astype(np.float64), axis, -1)
    blocks = v.reshape(v.shape[:-1] + (-1, 32))
    amax = np.abs(blocks).max(-1, keepdims=True)
    byte = np.maximum(np.where(amax > 0, np.frexp(amax)[1] - 1 + 127, 0) - down, 1)
    scale = np.exp2(byte - 127.0)
    codes = (blocks / scale).astype(np.float32).astype(dtype).astype(np.float64)
    return np.moveaxis((codes * scale).reshape(v.shape), -1, axis)


WIDE = False


def mx_kscale(k):
    if not WIDE:
        return np.ones(k)
    levels = np.array([10, -10, 5, -5, 0])
    a = np.random.permutation(np.resize(levels, k // 512 * 4)).reshape(k // 512, 4)
    idx = np.arange(k)
    return np.exp2(a[idx // 512, idx % 128 // 32])


BF16 = ml_dtypes.bfloat16


def bf(x):
    return np.asarray(x, np.float32).astype(BF16)


def f64(x):
    return np.asarray(x).astype(np.float64)


E2M1 = np.array([0.0, 0.5, 1.0, 1.5, 2.0, 3.0, 4.0, 6.0, -0.0, -0.5, -1.0, -1.5, -2.0, -3.0, -4.0, -6.0])


def pack_weight(w, fmt):
    k, n = w.shape
    w = f64(bf(w)).reshape(k // 32, 32, n)
    amax = np.abs(w).max(1)
    if fmt == "e4m3":
        byte = np.frexp(amax)[1] - 1 + 127 - 7
    else:
        mant, ex = np.frexp(amax / 6.0)
        byte = np.where(mant > 0.5, ex, ex - 1) + 127
    byte = np.clip(np.where(amax > 0, byte, 1), 1, 254)
    scaled = (w * np.exp2(127.0 - byte)[:, None, :]).reshape(k, n).astype(np.float32)
    by_word = np.ascontiguousarray(scaled.reshape(k // 512, 128, 4, n).transpose(0, 1, 3, 2))
    if fmt == "e4m3":
        words = by_word.astype(ml_dtypes.float8_e4m3fn).view(np.uint8)
    else:
        c = by_word.astype(ml_dtypes.float4_e2m1fn).view(np.uint8) & 0xF
        words = c[..., 0::2] | (c[..., 1::2] << 4)
    return np.ascontiguousarray(words), np.ascontiguousarray(byte.astype(np.uint8).reshape(k // 512, 16, n))


def unpack_weight(words, scales, fmt):
    g, p, n, _ = words.shape
    if fmt == "e4m3":
        vals = np.ascontiguousarray(words).view(ml_dtypes.float8_e4m3fn).astype(np.float64)
    else:
        nib = np.empty((g, p, n, 4), np.uint8)
        nib[..., 0::2] = words & 0xF
        nib[..., 1::2] = words >> 4
        vals = E2M1[nib]
    vals = vals * np.repeat(np.exp2(scales.astype(np.float64) - 127.0), 8, axis=1)[..., None]
    return vals.transpose(0, 1, 3, 2).reshape(g * 512, n)

def pack4(w):
    words, scales = pack_weight(w, "e2m1")
    return words.reshape(words.shape[0], 128, -1), scales


def unpack4(words, scales):
    return unpack_weight(words.reshape(words.shape[0], 128, -1, 2), scales, "e2m1")


T, K, E, H, KVH, D = 512, 1024, 2048, 16, 4, 128
EPS = 1e-05


def rmsnorm(x, w):
    var = np.mean(np.square(x), axis=-1, keepdims=True)
    return x * (1.0 / np.sqrt(var + EPS)) * w


def setup_inputs():
    s = mx_kscale(E)
    hidden_states = bf(np.random.standard_normal((T, E)) * s)
    wq = np.random.standard_normal((H * D, E)) / np.sqrt(E) / s
    words, scales = pack4(np.ascontiguousarray(wq.T))
    q_norm_w = bf(1.5 + 0.1 * np.random.standard_normal(D))
    return {"hidden_states": hidden_states,
            "Wq_words": words,
            "Wq_scales": scales,
            "q_norm_w": q_norm_w}


def reference(hidden_states, Wq_words, Wq_scales, q_norm_w):
    q = mxq(f64(hidden_states), 1, "e4m3") @ unpack4(Wq_words, Wq_scales)
    qh = rmsnorm(q.reshape(T, H, D), f64(q_norm_w))
    return qh.transpose(1, 0, 2)

@@ -1,0 +1,159 @@
+from contextlib import ExitStack
+
+import concourse.mybir as mybir
+from concourse.masks import make_identity
+
+F32 = mybir.dt.float32
+BF16 = mybir.dt.bfloat16
+I32 = mybir.dt.int32
+U32 = mybir.dt.uint32
+U8 = mybir.dt.uint8
+FP8X4 = mybir.dt.float8_e4m3fn_x4
+FP4X4 = mybir.dt.float4_e2m1fn_x4
+MULT = mybir.AluOpType.mult
+SQUARE = mybir.ActivationFunctionType.Square
+SQRT = mybir.ActivationFunctionType.Sqrt
+
+TOKENS, K, HEADS, HEAD_DIM = 512, 2048, 16, 128
+EPS = 1e-5
+
+P = 128
+K_PASS = 4 * P
+PASSES = K // K_PASS
+TOKEN_TILES = TOKENS // P
+BANK = 512
+N_TILE = BANK
+FEATURE_TILES = HEADS * HEAD_DIM // N_TILE
+HEADS_PER_TILE = N_TILE // HEAD_DIM
+WORDS_PER_PASS = K_PASS // 2
+
+FLOPS = 2 * TOKENS * K * HEADS * HEAD_DIM
+
+
+def tile_combcrossattention_pa_kernel(tc, hidden_states, Wq_words, Wq_scales, q_norm_w, out):
+    nc = tc.nc
+    with ExitStack() as ctx:
+        const = ctx.enter_context(tc.tile_pool(name="const", bufs=1))
+        keep = ctx.enter_context(tc.tile_pool(name="keep", bufs=1))
+        stats = ctx.enter_context(tc.tile_pool(name="stats", bufs=4))
+        results = ctx.enter_context(tc.tile_pool(name="results", bufs=FEATURE_TILES))
+        psum = ctx.enter_context(tc.psum_pool(name="psum", bufs=8))
+
+        identity = const.tile([P, P], F32)
+        make_identity(nc, identity[:])
+        ones = const.tile([P, P], BF16)
+        nc.vector.memset(ones[:], 1.0)
+        gain_rows = const.tile([P, HEAD_DIM], BF16)
+        nc.vector.memset(gain_rows[:], 0.0)
+        eps = const.tile([P, 1], F32)
+        nc.vector.memset(eps[:], EPS)
+        w_planes = keep.tile([P, PASSES, HEADS * HEAD_DIM], U8, align_bytes=64)
+        nc.vector.memset(w_planes[:].bitcast(I32), 0)
+        table_warmer = const.tile([P, 1], F32)
+        nc.scalar.activation(out=table_warmer[:], in_=eps[:], func=SQRT)
+
+        x_rows = []
+        x_by_tile = hidden_states.rearrange("(p j) k -> j p k", j=TOKEN_TILES)
+        for j in range(TOKEN_TILES):
+            x_rows.append(keep.tile([P, K], BF16, name="x_rows%d" % j))
+            nc.sync.dma_start(out=x_rows[j][:], in_=x_by_tile[j])
+        nc.scalar.dma_start(out=gain_rows[0:1, :], in_=q_norm_w.rearrange("(o d) -> o d", o=1))
+
+        scale_rows = Wq_scales.bitcast(I32).rearrange("g q c -> q g c")
+        for q in range(8):
+            partition = 32 * (q // 4) + q % 4
+            nc.sync.dma_start(out=w_planes[partition:P:64].bitcast(I32), in_=scale_rows[q:16:8])
+
+        w_words = []
+        words_by_partition = Wq_words.bitcast(I32).rearrange("g p c -> p g c")
+        int32_per_tile = 2 * N_TILE // 4
+        for n in range(FEATURE_TILES):
+            w_words.append(keep.tile([P, PASSES, 2 * N_TILE], U8, align_bytes=64, name="w_words%d" % n))
+            nc.sync.dma_start(
+                out=w_words[n][:].bitcast(I32),
+                in_=words_by_partition[:, :, n * int32_per_tile : (n + 1) * int32_per_tile],
+            )
+
+        grouped = []
+        x_codes = []
+        x_planes = []
+        for j in range(TOKEN_TILES):
+            grouped.append(keep.tile([P, PASSES * P * 4], BF16, align_bytes=64, name="grouped%d" % j))
+            x_codes.append(keep.tile([P, PASSES * P], U32, align_bytes=64, name="x_codes%d" % j))
+            x_planes.append(keep.tile([P, PASSES * P], U8, align_bytes=64, name="x_planes%d" % j))
+
+        def transpose_token_tile(j):
+            x_words = x_rows[j][:].bitcast(F32)
+            grouped_words = grouped[j][:].bitcast(F32)
+            for half in range(2):
+                bank = psum.tile([P, 2, 2, P], F32, tag="bank")
+                for gg in range(2):
+                    first = (2 * half + gg) * WORDS_PER_PASS
+                    for u in range(2):
+                        nc.tensor.transpose(
+                            bank[:, gg, u, :], x_words[:, first + u : first + WORDS_PER_PASS : 2], identity[:]
+                        )
+                copy_out = nc.vector.tensor_copy if half == 0 else nc.scalar.copy
+                copy_out(
+                    out=grouped_words[:, half * BANK : (half + 1) * BANK].rearrange(
+                        "p (g r u) -> p g r u", g=2, u=2
+                    ),
+                    in_=bank[:].rearrange("p g u r -> p g r u"),
+                )
+
+        def quantise_token_tile(j):
+            nc.vector.quantize_mx(out=x_codes[j][:].bitcast(FP8X4), scales=x_planes[j][:], in_=grouped[j][:])
+
+        for j in range(TOKEN_TILES):
+            transpose_token_tile(j)
+            if j > 0:
+                quantise_token_tile(j - 1)
+        quantise_token_tile(TOKEN_TILES - 1)
+
+        gain_bank = psum.tile([P, BANK], F32, tag="bank")
+        nc.tensor.matmul(out=gain_bank[:, 0:HEAD_DIM], lhsT=ones[:], rhs=gain_rows[:], start=True, stop=True)
+        gain = const.tile([P, HEAD_DIM], F32)
+        nc.vector.tensor_copy(out=gain[:], in_=gain_bank[:, 0:HEAD_DIM])
+
+        for n in range(FEATURE_TILES):
+            normed = results.tile([P, HEADS_PER_TILE, TOKEN_TILES, HEAD_DIM], F32)
+            for j in range(TOKEN_TILES):
+                q_bank = psum.tile([P, N_TILE], F32, tag="bank")
+                for g in range(PASSES):
+                    tokens = slice(g * P, (g + 1) * P)
+                    nc.tensor.matmul_mx(
+                        out=q_bank[:],
+                        lhsT=x_codes[j][:, tokens].bitcast(FP8X4),
+                        lhsT_scale=x_planes[j][:, tokens],
+                        rhs=w_words[n][:, g, :].bitcast(FP4X4),
+                        rhs_scale=w_planes[:, g, n * N_TILE : (n + 1) * N_TILE],
+                        start=(g == 0),
+                        stop=(g == PASSES - 1),
+                    )
+                sum_sq = stats.tile([P, HEADS_PER_TILE], F32)
+                for hh in range(HEADS_PER_TILE):
+                    squares = stats.tile([P, HEAD_DIM], BF16)
+                    nc.scalar.activation(
+                        out=squares[:],
+                        in_=q_bank[:, hh * HEAD_DIM : (hh + 1) * HEAD_DIM],
+                        func=SQUARE,
+                        accum_out=sum_sq[:, hh : hh + 1],
+                    )
+                rms = stats.tile([P, HEADS_PER_TILE], F32)
+                nc.scalar.activation(out=rms[:], in_=sum_sq[:], func=SQRT, scale=1.0 / HEAD_DIM, bias=eps[:])
+                inv_rms = stats.tile([P, HEADS_PER_TILE], F32)
+                nc.vector.reciprocal(out=inv_rms[:], in_=rms[:])
+                for hh in range(HEADS_PER_TILE):
+                    nc.vector.scalar_tensor_tensor(
+                        out=normed[:, hh, j, :],
+                        in0=q_bank[:, hh * HEAD_DIM : (hh + 1) * HEAD_DIM],
+                        scalar=inv_rms[:, hh : hh + 1],
+                        in1=gain[:],
+                        op0=MULT,
+                        op1=MULT,
+                    )
+            for hh in range(HEADS_PER_TILE):
+                nc.sync.dma_start(
+                    out=out[n * HEADS_PER_TILE + hh].rearrange("(p j) d -> p j d", j=TOKEN_TILES),
+                    in_=normed[:, hh, :, :],
+                )

@@ -12,7 +12,7 @@ FP8X4 = mybir.dt.float8_e4m3fn_x4
 FP4X4 = mybir.dt.float4_e2m1fn_x4
 MULT = mybir.AluOpType.mult
 SQUARE = mybir.ActivationFunctionType.Square
-SQRT = mybir.ActivationFunctionType.Sqrt
+INV_SQRT = mybir.ActivationFunctionType.Abs_reciprocal_sqrt
 
 TOKENS, K, HEADS, HEAD_DIM = 512, 2048, 16, 128
 EPS = 1e-5
@@ -38,6 +38,7 @@ def tile_combcrossattention_pa_kernel(tc, hidden_states, Wq_words, Wq_scales, q_
         stats = ctx.enter_context(tc.tile_pool(name="stats", bufs=4))
         results = ctx.enter_context(tc.tile_pool(name="results", bufs=FEATURE_TILES))
         psum = ctx.enter_context(tc.psum_pool(name="psum", bufs=8))
+        ctx.enter_context(tc.manual_schedule())
 
         identity = const.tile([P, P], F32)
         make_identity(nc, identity[:])
@@ -45,19 +46,19 @@ def tile_combcrossattention_pa_kernel(tc, hidden_states, Wq_words, Wq_scales, q_
         nc.vector.memset(ones[:], 1.0)
         gain_rows = const.tile([P, HEAD_DIM], BF16)
         nc.vector.memset(gain_rows[:], 0.0)
+        nc.scalar.dma_start(out=gain_rows[0:1, :], in_=q_norm_w.rearrange("(o d) -> o d", o=1))
         eps = const.tile([P, 1], F32)
         nc.vector.memset(eps[:], EPS)
         w_planes = keep.tile([P, PASSES, HEADS * HEAD_DIM], U8, align_bytes=64)
         nc.vector.memset(w_planes[:].bitcast(I32), 0)
         table_warmer = const.tile([P, 1], F32)
-        nc.scalar.activation(out=table_warmer[:], in_=eps[:], func=SQRT)
+        nc.scalar.activation(out=table_warmer[:], in_=eps[:], func=INV_SQRT)
 
         x_rows = []
         x_by_tile = hidden_states.rearrange("(p j) k -> j p k", j=TOKEN_TILES)
         for j in range(TOKEN_TILES):
             x_rows.append(keep.tile([P, K], BF16, name="x_rows%d" % j))
             nc.sync.dma_start(out=x_rows[j][:], in_=x_by_tile[j])
-        nc.scalar.dma_start(out=gain_rows[0:1, :], in_=q_norm_w.rearrange("(o d) -> o d", o=1))
 
         scale_rows = Wq_scales.bitcast(I32).rearrange("g q c -> q g c")
         for q in range(8):
@@ -115,45 +116,61 @@ def tile_combcrossattention_pa_kernel(tc, hidden_states, Wq_words, Wq_scales, q_
         gain = const.tile([P, HEAD_DIM], F32)
         nc.vector.tensor_copy(out=gain[:], in_=gain_bank[:, 0:HEAD_DIM])
 
+        normed = []
         for n in range(FEATURE_TILES):
-            normed = results.tile([P, HEADS_PER_TILE, TOKEN_TILES, HEAD_DIM], F32)
-            for j in range(TOKEN_TILES):
-                q_bank = psum.tile([P, N_TILE], F32, tag="bank")
-                for g in range(PASSES):
-                    tokens = slice(g * P, (g + 1) * P)
-                    nc.tensor.matmul_mx(
-                        out=q_bank[:],
-                        lhsT=x_codes[j][:, tokens].bitcast(FP8X4),
-                        lhsT_scale=x_planes[j][:, tokens],
-                        rhs=w_words[n][:, g, :].bitcast(FP4X4),
-                        rhs_scale=w_planes[:, g, n * N_TILE : (n + 1) * N_TILE],
-                        start=(g == 0),
-                        stop=(g == PASSES - 1),
-                    )
-                sum_sq = stats.tile([P, HEADS_PER_TILE], F32)
-                for hh in range(HEADS_PER_TILE):
-                    squares = stats.tile([P, HEAD_DIM], BF16)
-                    nc.scalar.activation(
-                        out=squares[:],
-                        in_=q_bank[:, hh * HEAD_DIM : (hh + 1) * HEAD_DIM],
-                        func=SQUARE,
-                        accum_out=sum_sq[:, hh : hh + 1],
-                    )
-                rms = stats.tile([P, HEADS_PER_TILE], F32)
-                nc.scalar.activation(out=rms[:], in_=sum_sq[:], func=SQRT, scale=1.0 / HEAD_DIM, bias=eps[:])
-                inv_rms = stats.tile([P, HEADS_PER_TILE], F32)
-                nc.vector.reciprocal(out=inv_rms[:], in_=rms[:])
-                for hh in range(HEADS_PER_TILE):
-                    nc.vector.scalar_tensor_tensor(
-                        out=normed[:, hh, j, :],
-                        in0=q_bank[:, hh * HEAD_DIM : (hh + 1) * HEAD_DIM],
-                        scalar=inv_rms[:, hh : hh + 1],
-                        in1=gain[:],
-                        op0=MULT,
-                        op1=MULT,
-                    )
-            for hh in range(HEADS_PER_TILE):
-                nc.sync.dma_start(
-                    out=out[n * HEADS_PER_TILE + hh].rearrange("(p j) d -> p j d", j=TOKEN_TILES),
-                    in_=normed[:, hh, :, :],
+            normed.append(results.tile([P, HEADS_PER_TILE, TOKEN_TILES, HEAD_DIM], F32, name="normed", tag="normed"))
+
+        def project(n, j):
+            q_bank = psum.tile([P, N_TILE], F32, tag="bank")
+            for g in range(PASSES):
+                tokens = slice(g * P, (g + 1) * P)
+                nc.tensor.matmul_mx(
+                    out=q_bank[:],
+                    lhsT=x_codes[j][:, tokens].bitcast(FP8X4),
+                    lhsT_scale=x_planes[j][:, tokens],
+                    rhs=w_words[n][:, g, :].bitcast(FP4X4),
+                    rhs_scale=w_planes[:, g, n * N_TILE : (n + 1) * N_TILE],
+                    start=(g == 0),
+                    stop=(g == PASSES - 1),
                 )
+            return q_bank
+
+        def sum_squares(q_bank, sum_sq, hh):
+            squares = stats.tile([P, HEAD_DIM], BF16)
+            nc.scalar.activation(
+                out=squares[:],
+                in_=q_bank[:, hh * HEAD_DIM : (hh + 1) * HEAD_DIM],
+                func=SQUARE,
+                accum_out=sum_sq[:, hh : hh + 1],
+            )
+
+        def normalise(n, j, q_bank, sum_sq):
+            inv_rms = stats.tile([P, HEADS_PER_TILE], F32)
+            nc.scalar.activation(out=inv_rms[:], in_=sum_sq[:], func=INV_SQRT, scale=1.0 / HEAD_DIM, bias=eps[:])
+            for hh in range(HEADS_PER_TILE):
+                nc.vector.scalar_tensor_tensor(
+                    out=normed[n][:, hh, j, :],
+                    in0=q_bank[:, hh * HEAD_DIM : (hh + 1) * HEAD_DIM],
+                    scalar=inv_rms[:, hh : hh + 1],
+                    in1=gain[:],
+                    op0=MULT,
+                    op1=MULT,
+                )
+                if j == TOKEN_TILES - 1:
+                    nc.sync.dma_start(
+                        out=out[n * HEADS_PER_TILE + hh].rearrange("(p j) d -> p j d", j=TOKEN_TILES),
+                        in_=normed[n][:, hh, :, :],
+                    )
+
+        waiting = None
+        for n in range(FEATURE_TILES):
+            for j in range(TOKEN_TILES):
+                q_bank = project(n, j)
+                sum_sq = stats.tile([P, HEADS_PER_TILE], F32)
+                sum_squares(q_bank, sum_sq, 0)
+                if waiting is not None:
+                    normalise(*waiting)
+                for hh in range(1, HEADS_PER_TILE):
+                    sum_squares(q_bank, sum_sq, hh)
+                waiting = (n, j, q_bank, sum_sq)
+        normalise(*waiting)

@@ -38,7 +38,6 @@ def tile_combcrossattention_pa_kernel(tc, hidden_states, Wq_words, Wq_scales, q_
         stats = ctx.enter_context(tc.tile_pool(name="stats", bufs=4))
         results = ctx.enter_context(tc.tile_pool(name="results", bufs=FEATURE_TILES))
         psum = ctx.enter_context(tc.psum_pool(name="psum", bufs=8))
-        ctx.enter_context(tc.manual_schedule())
 
         identity = const.tile([P, P], F32)
         make_identity(nc, identity[:])
@@ -49,8 +48,10 @@ def tile_combcrossattention_pa_kernel(tc, hidden_states, Wq_words, Wq_scales, q_
         nc.scalar.dma_start(out=gain_rows[0:1, :], in_=q_norm_w.rearrange("(o d) -> o d", o=1))
         eps = const.tile([P, 1], F32)
         nc.vector.memset(eps[:], EPS)
-        w_planes = keep.tile([P, PASSES, HEADS * HEAD_DIM], U8, align_bytes=64)
-        nc.vector.memset(w_planes[:].bitcast(I32), 0)
+        w_planes = []
+        for n in range(FEATURE_TILES):
+            w_planes.append(keep.tile([P, PASSES, N_TILE], U8, align_bytes=64, name="w_planes%d" % n))
+            nc.vector.memset(w_planes[n][:].bitcast(I32), 0)
         table_warmer = const.tile([P, 1], F32)
         nc.scalar.activation(out=table_warmer[:], in_=eps[:], func=INV_SQRT)
 
@@ -60,20 +61,16 @@ def tile_combcrossattention_pa_kernel(tc, hidden_states, Wq_words, Wq_scales, q_
             x_rows.append(keep.tile([P, K], BF16, name="x_rows%d" % j))
             nc.sync.dma_start(out=x_rows[j][:], in_=x_by_tile[j])
 
-        scale_rows = Wq_scales.bitcast(I32).rearrange("g q c -> q g c")
-        for q in range(8):
-            partition = 32 * (q // 4) + q % 4
-            nc.sync.dma_start(out=w_planes[partition:P:64].bitcast(I32), in_=scale_rows[q:16:8])
-
         w_words = []
+        scale_rows = Wq_scales.bitcast(I32).rearrange("g q c -> q g c")
         words_by_partition = Wq_words.bitcast(I32).rearrange("g p c -> p g c")
-        int32_per_tile = 2 * N_TILE // 4
         for n in range(FEATURE_TILES):
+            scale_cols = slice(n * N_TILE // 4, (n + 1) * N_TILE // 4)
+            for r in range(4):
+                nc.sync.dma_start(out=w_planes[n][r:P:32].bitcast(I32), in_=scale_rows[r:16:4, :, scale_cols])
+            word_cols = slice(n * N_TILE // 2, (n + 1) * N_TILE // 2)
             w_words.append(keep.tile([P, PASSES, 2 * N_TILE], U8, align_bytes=64, name="w_words%d" % n))
-            nc.sync.dma_start(
-                out=w_words[n][:].bitcast(I32),
-                in_=words_by_partition[:, :, n * int32_per_tile : (n + 1) * int32_per_tile],
-            )
+            nc.sync.dma_start(out=w_words[n][:].bitcast(I32), in_=words_by_partition[:, :, word_cols])
 
         grouped = []
         x_codes = []
@@ -116,61 +113,43 @@ def tile_combcrossattention_pa_kernel(tc, hidden_states, Wq_words, Wq_scales, q_
         gain = const.tile([P, HEAD_DIM], F32)
         nc.vector.tensor_copy(out=gain[:], in_=gain_bank[:, 0:HEAD_DIM])
 
-        normed = []
         for n in range(FEATURE_TILES):
-            normed.append(results.tile([P, HEADS_PER_TILE, TOKEN_TILES, HEAD_DIM], F32, name="normed", tag="normed"))
-
-        def project(n, j):
-            q_bank = psum.tile([P, N_TILE], F32, tag="bank")
-            for g in range(PASSES):
-                tokens = slice(g * P, (g + 1) * P)
-                nc.tensor.matmul_mx(
-                    out=q_bank[:],
-                    lhsT=x_codes[j][:, tokens].bitcast(FP8X4),
-                    lhsT_scale=x_planes[j][:, tokens],
-                    rhs=w_words[n][:, g, :].bitcast(FP4X4),
-                    rhs_scale=w_planes[:, g, n * N_TILE : (n + 1) * N_TILE],
-                    start=(g == 0),
-                    stop=(g == PASSES - 1),
-                )
-            return q_bank
-
-        def sum_squares(q_bank, sum_sq, hh):
-            squares = stats.tile([P, HEAD_DIM], BF16)
-            nc.scalar.activation(
-                out=squares[:],
-                in_=q_bank[:, hh * HEAD_DIM : (hh + 1) * HEAD_DIM],
-                func=SQUARE,
-                accum_out=sum_sq[:, hh : hh + 1],
-            )
-
-        def normalise(n, j, q_bank, sum_sq):
-            inv_rms = stats.tile([P, HEADS_PER_TILE], F32)
-            nc.scalar.activation(out=inv_rms[:], in_=sum_sq[:], func=INV_SQRT, scale=1.0 / HEAD_DIM, bias=eps[:])
-            for hh in range(HEADS_PER_TILE):
-                nc.vector.scalar_tensor_tensor(
-                    out=normed[n][:, hh, j, :],
-                    in0=q_bank[:, hh * HEAD_DIM : (hh + 1) * HEAD_DIM],
-                    scalar=inv_rms[:, hh : hh + 1],
-                    in1=gain[:],
-                    op0=MULT,
-                    op1=MULT,
-                )
-                if j == TOKEN_TILES - 1:
-                    nc.sync.dma_start(
-                        out=out[n * HEADS_PER_TILE + hh].rearrange("(p j) d -> p j d", j=TOKEN_TILES),
-                        in_=normed[n][:, hh, :, :],
-                    )
-
-        waiting = None
-        for n in range(FEATURE_TILES):
+            normed = results.tile([P, HEADS_PER_TILE, TOKEN_TILES, HEAD_DIM], F32)
             for j in range(TOKEN_TILES):
-                q_bank = project(n, j)
+                q_bank = psum.tile([P, N_TILE], F32, tag="bank")
+                for g in range(PASSES):
+                    tokens = slice(g * P, (g + 1) * P)
+                    nc.tensor.matmul_mx(
+                        out=q_bank[:],
+                        lhsT=x_codes[j][:, tokens].bitcast(FP8X4),
+                        lhsT_scale=x_planes[j][:, tokens],
+                        rhs=w_words[n][:, g, :].bitcast(FP4X4),
+                        rhs_scale=w_planes[n][:, g, :],
+                        start=(g == 0),
+                        stop=(g == PASSES - 1),
+                    )
                 sum_sq = stats.tile([P, HEADS_PER_TILE], F32)
-                sum_squares(q_bank, sum_sq, 0)
-                if waiting is not None:
-                    normalise(*waiting)
-                for hh in range(1, HEADS_PER_TILE):
-                    sum_squares(q_bank, sum_sq, hh)
-                waiting = (n, j, q_bank, sum_sq)
-        normalise(*waiting)
+                for hh in range(HEADS_PER_TILE):
+                    squares = stats.tile([P, HEAD_DIM], BF16)
+                    nc.scalar.activation(
+                        out=squares[:],
+                        in_=q_bank[:, hh * HEAD_DIM : (hh + 1) * HEAD_DIM],
+                        func=SQUARE,
+                        accum_out=sum_sq[:, hh : hh + 1],
+                    )
+                inv_rms = stats.tile([P, HEADS_PER_TILE], F32)
+                nc.scalar.activation(out=inv_rms[:], in_=sum_sq[:], func=INV_SQRT, scale=1.0 / HEAD_DIM, bias=eps[:])
+                for hh in range(HEADS_PER_TILE):
+                    nc.vector.scalar_tensor_tensor(
+                        out=normed[:, hh, j, :],
+                        in0=q_bank[:, hh * HEAD_DIM : (hh + 1) * HEAD_DIM],
+                        scalar=inv_rms[:, hh : hh + 1],
+                        in1=gain[:],
+                        op0=MULT,
+                        op1=MULT,
+                    )
+                    head_rows = out[n * HEADS_PER_TILE + hh].rearrange("(p j) d -> p j d", j=TOKEN_TILES)
+                    if n == FEATURE_TILES - 1:
+                        nc.sync.dma_start(out=head_rows[:, j, :], in_=normed[:, hh, j, :])
+                    elif j == TOKEN_TILES - 1:
+                        nc.sync.dma_start(out=head_rows, in_=normed[:, hh, :, :])

@@ -26,6 +26,7 @@ N_TILE = BANK
 FEATURE_TILES = HEADS * HEAD_DIM // N_TILE
 HEADS_PER_TILE = N_TILE // HEAD_DIM
 WORDS_PER_PASS = K_PASS // 2
+PASSES_PER_LOAD = 2
 
 FLOPS = 2 * TOKENS * K * HEADS * HEAD_DIM
 
@@ -69,8 +70,16 @@ def tile_combcrossattention_pa_kernel(tc, hidden_states, Wq_words, Wq_scales, q_
             for r in range(4):
                 nc.sync.dma_start(out=w_planes[n][r:P:32].bitcast(I32), in_=scale_rows[r:16:4, :, scale_cols])
             word_cols = slice(n * N_TILE // 2, (n + 1) * N_TILE // 2)
-            w_words.append(keep.tile([P, PASSES, 2 * N_TILE], U8, align_bytes=64, name="w_words%d" % n))
-            nc.sync.dma_start(out=w_words[n][:].bitcast(I32), in_=words_by_partition[:, :, word_cols])
+            w_words.append([])
+            for first_pass in range(0, PASSES, PASSES_PER_LOAD):
+                words = keep.tile(
+                    [P, PASSES_PER_LOAD, 2 * N_TILE], U8, align_bytes=64, name="w_words%d_%d" % (n, first_pass)
+                )
+                nc.sync.dma_start(
+                    out=words[:].bitcast(I32),
+                    in_=words_by_partition[:, first_pass : first_pass + PASSES_PER_LOAD, word_cols],
+                )
+                w_words[n].append(words)
 
         grouped = []
         x_codes = []
@@ -123,7 +132,7 @@ def tile_combcrossattention_pa_kernel(tc, hidden_states, Wq_words, Wq_scales, q_
                         out=q_bank[:],
                         lhsT=x_codes[j][:, tokens].bitcast(FP8X4),
                         lhsT_scale=x_planes[j][:, tokens],
-                        rhs=w_words[n][:, g, :].bitcast(FP4X4),
+                        rhs=w_words[n][g // PASSES_PER_LOAD][:, g % PASSES_PER_LOAD, :].bitcast(FP4X4),
                         rhs_scale=w_planes[n][:, g, :],
                         start=(g == 0),
                         stop=(g == PASSES - 1),

@@ -26,7 +26,7 @@ N_TILE = BANK
 FEATURE_TILES = HEADS * HEAD_DIM // N_TILE
 HEADS_PER_TILE = N_TILE // HEAD_DIM
 WORDS_PER_PASS = K_PASS // 2
-PASSES_PER_LOAD = 2
+PASSES_PER_LOAD = 1
 
 FLOPS = 2 * TOKENS * K * HEADS * HEAD_DIM
 

@@ -122,43 +122,64 @@ def tile_combcrossattention_pa_kernel(tc, hidden_states, Wq_words, Wq_scales, q_
         gain = const.tile([P, HEAD_DIM], F32)
         nc.vector.tensor_copy(out=gain[:], in_=gain_bank[:, 0:HEAD_DIM])
 
+        def project(n, j, first_head, head_count):
+            width = head_count * HEAD_DIM
+            first = first_head * HEAD_DIM
+            q_bank = psum.tile([P, width], F32, tag="bank")
+            for g in range(PASSES):
+                tokens = slice(g * P, (g + 1) * P)
+                nc.tensor.matmul_mx(
+                    out=q_bank[:],
+                    lhsT=x_codes[j][:, tokens].bitcast(FP8X4),
+                    lhsT_scale=x_planes[j][:, tokens],
+                    rhs=w_words[n][g // PASSES_PER_LOAD][
+                        :, g % PASSES_PER_LOAD, 2 * first : 2 * (first + width)
+                    ].bitcast(FP4X4),
+                    rhs_scale=w_planes[n][:, g, first : first + width],
+                    start=(g == 0),
+                    stop=(g == PASSES - 1),
+                )
+            return q_bank
+
+        def normalise(n, j, first_head, head_count, q_bank, normed):
+            sum_sq = stats.tile([P, HEADS_PER_TILE], F32)
+            for i in range(head_count):
+                squares = stats.tile([P, HEAD_DIM], BF16)
+                nc.scalar.activation(
+                    out=squares[:],
+                    in_=q_bank[:, i * HEAD_DIM : (i + 1) * HEAD_DIM],
+                    func=SQUARE,
+                    accum_out=sum_sq[:, i : i + 1],
+                )
+            inv_rms = stats.tile([P, HEADS_PER_TILE], F32)
+            nc.scalar.activation(
+                out=inv_rms[:, 0:head_count],
+                in_=sum_sq[:, 0:head_count],
+                func=INV_SQRT,
+                scale=1.0 / HEAD_DIM,
+                bias=eps[:],
+            )
+            for i in range(head_count):
+                hh = first_head + i
+                nc.vector.scalar_tensor_tensor(
+                    out=normed[:, hh, j, :],
+                    in0=q_bank[:, i * HEAD_DIM : (i + 1) * HEAD_DIM],
+                    scalar=inv_rms[:, i : i + 1],
+                    in1=gain[:],
+                    op0=MULT,
+                    op1=MULT,
+                )
+                head_rows = out[n * HEADS_PER_TILE + hh].rearrange("(p j) d -> p j d", j=TOKEN_TILES)
+                if n == FEATURE_TILES - 1:
+                    nc.sync.dma_start(out=head_rows[:, j, :], in_=normed[:, hh, j, :])
+                elif j == TOKEN_TILES - 1:
+                    nc.sync.dma_start(out=head_rows, in_=normed[:, hh, :, :])
+
         for n in range(FEATURE_TILES):
             normed = results.tile([P, HEADS_PER_TILE, TOKEN_TILES, HEAD_DIM], F32)
             for j in range(TOKEN_TILES):
-                q_bank = psum.tile([P, N_TILE], F32, tag="bank")
-                for g in range(PASSES):
-                    tokens = slice(g * P, (g + 1) * P)
-                    nc.tensor.matmul_mx(
-                        out=q_bank[:],
-                        lhsT=x_codes[j][:, tokens].bitcast(FP8X4),
-                        lhsT_scale=x_planes[j][:, tokens],
-                        rhs=w_words[n][g // PASSES_PER_LOAD][:, g % PASSES_PER_LOAD, :].bitcast(FP4X4),
-                        rhs_scale=w_planes[n][:, g, :],
-                        start=(g == 0),
-                        stop=(g == PASSES - 1),
-                    )
-                sum_sq = stats.tile([P, HEADS_PER_TILE], F32)
-                for hh in range(HEADS_PER_TILE):
-                    squares = stats.tile([P, HEAD_DIM], BF16)
-                    nc.scalar.activation(
-                        out=squares[:],
-                        in_=q_bank[:, hh * HEAD_DIM : (hh + 1) * HEAD_DIM],
-                        func=SQUARE,
-                        accum_out=sum_sq[:, hh : hh + 1],
-                    )
-                inv_rms = stats.tile([P, HEADS_PER_TILE], F32)
-                nc.scalar.activation(out=inv_rms[:], in_=sum_sq[:], func=INV_SQRT, scale=1.0 / HEAD_DIM, bias=eps[:])
-                for hh in range(HEADS_PER_TILE):
-                    nc.vector.scalar_tensor_tensor(
-                        out=normed[:, hh, j, :],
-                        in0=q_bank[:, hh * HEAD_DIM : (hh + 1) * HEAD_DIM],
-                        scalar=inv_rms[:, hh : hh + 1],
-                        in1=gain[:],
-                        op0=MULT,
-                        op1=MULT,
-                    )
-                    head_rows = out[n * HEADS_PER_TILE + hh].rearrange("(p j) d -> p j d", j=TOKEN_TILES)
-                    if n == FEATURE_TILES - 1:
-                        nc.sync.dma_start(out=head_rows[:, j, :], in_=normed[:, hh, j, :])
-                    elif j == TOKEN_TILES - 1:
-                        nc.sync.dma_start(out=head_rows, in_=normed[:, hh, :, :])
+                if n == FEATURE_TILES - 1 and j == TOKEN_TILES - 1:
+                    for hh in range(HEADS_PER_TILE):
+                        normalise(n, j, hh, 1, project(n, j, hh, 1), normed)
+                else:
+                    normalise(n, j, 0, HEADS_PER_TILE, project(n, j, 0, HEADS_PER_TILE), normed)

@@ -27,6 +27,8 @@ FEATURE_TILES = HEADS * HEAD_DIM // N_TILE
 HEADS_PER_TILE = N_TILE // HEAD_DIM
 WORDS_PER_PASS = K_PASS // 2
 PASSES_PER_LOAD = 1
+K_HALF = K // 2
+LATE_TILE = TOKEN_TILES - 1
 
 FLOPS = 2 * TOKENS * K * HEADS * HEAD_DIM
 
@@ -39,6 +41,7 @@ def tile_combcrossattention_pa_kernel(tc, hidden_states, Wq_words, Wq_scales, q_
         stats = ctx.enter_context(tc.tile_pool(name="stats", bufs=4))
         results = ctx.enter_context(tc.tile_pool(name="results", bufs=FEATURE_TILES))
         psum = ctx.enter_context(tc.psum_pool(name="psum", bufs=8))
+        ctx.enter_context(tc.manual_schedule(engines={mybir.EngineType.PE}))
 
         identity = const.tile([P, P], F32)
         make_identity(nc, identity[:])
@@ -58,14 +61,19 @@ def tile_combcrossattention_pa_kernel(tc, hidden_states, Wq_words, Wq_scales, q_
 
         x_rows = []
         x_by_tile = hidden_states.rearrange("(p j) k -> j p k", j=TOKEN_TILES)
-        for j in range(TOKEN_TILES):
-            x_rows.append(keep.tile([P, K], BF16, name="x_rows%d" % j))
-            nc.sync.dma_start(out=x_rows[j][:], in_=x_by_tile[j])
+
+        def load_x(j):
+            x_rows.append([])
+            for half in range(2):
+                rows = keep.tile([P, K_HALF], BF16, name="x_rows%d_%d" % (j, half))
+                nc.sync.dma_start(out=rows[:], in_=x_by_tile[j][:, half * K_HALF : (half + 1) * K_HALF])
+                x_rows[j].append(rows)
 
         w_words = []
         scale_rows = Wq_scales.bitcast(I32).rearrange("g q c -> q g c")
         words_by_partition = Wq_words.bitcast(I32).rearrange("g p c -> p g c")
-        for n in range(FEATURE_TILES):
+
+        def load_w(n):
             scale_cols = slice(n * N_TILE // 4, (n + 1) * N_TILE // 4)
             for r in range(4):
                 nc.sync.dma_start(out=w_planes[n][r:P:32].bitcast(I32), in_=scale_rows[r:16:4, :, scale_cols])
@@ -81,41 +89,44 @@ def tile_combcrossattention_pa_kernel(tc, hidden_states, Wq_words, Wq_scales, q_
                 )
                 w_words[n].append(words)
 
-        grouped = []
+        load_x(0)
+        load_x(1)
+        load_x(2)
+        load_w(0)
+        load_x(3)
+        load_w(1)
+        load_w(2)
+        load_w(3)
+
         x_codes = []
         x_planes = []
-        for j in range(TOKEN_TILES):
-            grouped.append(keep.tile([P, PASSES * P * 4], BF16, align_bytes=64, name="grouped%d" % j))
-            x_codes.append(keep.tile([P, PASSES * P], U32, align_bytes=64, name="x_codes%d" % j))
-            x_planes.append(keep.tile([P, PASSES * P], U8, align_bytes=64, name="x_planes%d" % j))
 
-        def transpose_token_tile(j):
-            x_words = x_rows[j][:].bitcast(F32)
-            grouped_words = grouped[j][:].bitcast(F32)
+        def prepare_x(j):
+            x_codes.append([])
+            x_planes.append([])
             for half in range(2):
+                x_words = x_rows[j][half][:].bitcast(F32)
                 bank = psum.tile([P, 2, 2, P], F32, tag="bank")
                 for gg in range(2):
-                    first = (2 * half + gg) * WORDS_PER_PASS
+                    first = gg * WORDS_PER_PASS
                     for u in range(2):
                         nc.tensor.transpose(
                             bank[:, gg, u, :], x_words[:, first + u : first + WORDS_PER_PASS : 2], identity[:]
                         )
-                copy_out = nc.vector.tensor_copy if half == 0 else nc.scalar.copy
+                grouped = keep.tile([P, 2 * P * 4], BF16, align_bytes=64, name="grouped%d_%d" % (j, half))
+                copy_out = nc.scalar.copy if j == LATE_TILE or half == 1 else nc.vector.tensor_copy
                 copy_out(
-                    out=grouped_words[:, half * BANK : (half + 1) * BANK].rearrange(
-                        "p (g r u) -> p g r u", g=2, u=2
-                    ),
+                    out=grouped[:].bitcast(F32).rearrange("p (g r u) -> p g r u", g=2, u=2),
                     in_=bank[:].rearrange("p g u r -> p g r u"),
                 )
+                codes = keep.tile([P, 2 * P], U32, align_bytes=64, name="x_codes%d_%d" % (j, half))
+                planes = keep.tile([P, 2 * P], U8, align_bytes=64, name="x_planes%d_%d" % (j, half))
+                nc.vector.quantize_mx(out=codes[:].bitcast(FP8X4), scales=planes[:], in_=grouped[:])
+                x_codes[j].append(codes)
+                x_planes[j].append(planes)
 
-        def quantise_token_tile(j):
-            nc.vector.quantize_mx(out=x_codes[j][:].bitcast(FP8X4), scales=x_planes[j][:], in_=grouped[j][:])
-
-        for j in range(TOKEN_TILES):
-            transpose_token_tile(j)
-            if j > 0:
-                quantise_token_tile(j - 1)
-        quantise_token_tile(TOKEN_TILES - 1)
+        for j in range(LATE_TILE):
+            prepare_x(j)
 
         gain_bank = psum.tile([P, BANK], F32, tag="bank")
         nc.tensor.matmul(out=gain_bank[:, 0:HEAD_DIM], lhsT=ones[:], rhs=gain_rows[:], start=True, stop=True)
@@ -127,11 +138,11 @@ def tile_combcrossattention_pa_kernel(tc, hidden_states, Wq_words, Wq_scales, q_
             first = first_head * HEAD_DIM
             q_bank = psum.tile([P, width], F32, tag="bank")
             for g in range(PASSES):
-                tokens = slice(g * P, (g + 1) * P)
+                tokens = slice((g % 2) * P, (g % 2 + 1) * P)
                 nc.tensor.matmul_mx(
                     out=q_bank[:],
-                    lhsT=x_codes[j][:, tokens].bitcast(FP8X4),
-                    lhsT_scale=x_planes[j][:, tokens],
+                    lhsT=x_codes[j][g // 2][:, tokens].bitcast(FP8X4),
+                    lhsT_scale=x_planes[j][g // 2][:, tokens],
                     rhs=w_words[n][g // PASSES_PER_LOAD][
                         :, g % PASSES_PER_LOAD, 2 * first : 2 * (first + width)
                     ].bitcast(FP4X4),
@@ -175,11 +186,12 @@ def tile_combcrossattention_pa_kernel(tc, hidden_states, Wq_words, Wq_scales, q_
                 elif j == TOKEN_TILES - 1:
                     nc.sync.dma_start(out=head_rows, in_=normed[:, hh, :, :])
 
+        def whole_bank(n, j, normed):
+            normalise(n, j, 0, HEADS_PER_TILE, project(n, j, 0, HEADS_PER_TILE), normed)
+
         for n in range(FEATURE_TILES):
             normed = results.tile([P, HEADS_PER_TILE, TOKEN_TILES, HEAD_DIM], F32)
             for j in range(TOKEN_TILES):
-                if n == FEATURE_TILES - 1 and j == TOKEN_TILES - 1:
-                    for hh in range(HEADS_PER_TILE):
-                        normalise(n, j, hh, 1, project(n, j, hh, 1), normed)
-                else:
-                    normalise(n, j, 0, HEADS_PER_TILE, project(n, j, 0, HEADS_PER_TILE), normed)
+                if n == 0 and j == 1:
+                    prepare_x(LATE_TILE)
+                whole_bank(n, j, normed)

@@ -26,9 +26,8 @@ N_TILE = BANK
 FEATURE_TILES = HEADS * HEAD_DIM // N_TILE
 HEADS_PER_TILE = N_TILE // HEAD_DIM
 WORDS_PER_PASS = K_PASS // 2
-PASSES_PER_LOAD = 1
+PASSES_TOGETHER = [2, 4, 4, 4]
 K_HALF = K // 2
-LATE_TILE = TOKEN_TILES - 1
 
 FLOPS = 2 * TOKENS * K * HEADS * HEAD_DIM
 
@@ -52,10 +51,15 @@ def tile_combcrossattention_pa_kernel(tc, hidden_states, Wq_words, Wq_scales, q_
         nc.scalar.dma_start(out=gain_rows[0:1, :], in_=q_norm_w.rearrange("(o d) -> o d", o=1))
         eps = const.tile([P, 1], F32)
         nc.vector.memset(eps[:], EPS)
-        w_planes = []
+        plane_tiles = []
         for n in range(FEATURE_TILES):
-            w_planes.append(keep.tile([P, PASSES, N_TILE], U8, align_bytes=64, name="w_planes%d" % n))
-            nc.vector.memset(w_planes[n][:].bitcast(I32), 0)
+            plane_tiles.append([])
+            for first_pass in range(0, PASSES, PASSES_TOGETHER[n]):
+                planes = keep.tile(
+                    [P, PASSES_TOGETHER[n], N_TILE], U8, align_bytes=64, name="w_planes%d_%d" % (n, first_pass)
+                )
+                nc.vector.memset(planes[:].bitcast(I32), 0)
+                plane_tiles[n].append(planes)
         table_warmer = const.tile([P, 1], F32)
         nc.scalar.activation(out=table_warmer[:], in_=eps[:], func=INV_SQRT)
 
@@ -73,30 +77,31 @@ def tile_combcrossattention_pa_kernel(tc, hidden_states, Wq_words, Wq_scales, q_
         scale_rows = Wq_scales.bitcast(I32).rearrange("g q c -> q g c")
         words_by_partition = Wq_words.bitcast(I32).rearrange("g p c -> p g c")
 
+        w_planes = []
+
         def load_w(n):
             scale_cols = slice(n * N_TILE // 4, (n + 1) * N_TILE // 4)
-            for r in range(4):
-                nc.sync.dma_start(out=w_planes[n][r:P:32].bitcast(I32), in_=scale_rows[r:16:4, :, scale_cols])
             word_cols = slice(n * N_TILE // 2, (n + 1) * N_TILE // 2)
             w_words.append([])
-            for first_pass in range(0, PASSES, PASSES_PER_LOAD):
-                words = keep.tile(
-                    [P, PASSES_PER_LOAD, 2 * N_TILE], U8, align_bytes=64, name="w_words%d_%d" % (n, first_pass)
-                )
-                nc.sync.dma_start(
-                    out=words[:].bitcast(I32),
-                    in_=words_by_partition[:, first_pass : first_pass + PASSES_PER_LOAD, word_cols],
-                )
-                w_words[n].append(words)
+            w_planes.append([])
+            together = PASSES_TOGETHER[n]
+            for first_pass in range(0, PASSES, together):
+                planes = plane_tiles[n][first_pass // together]
+                for r in range(4):
+                    nc.sync.dma_start(
+                        out=planes[r:P:32].bitcast(I32),
+                        in_=scale_rows[r:16:4, first_pass : first_pass + together, scale_cols],
+                    )
+                for g in range(first_pass, first_pass + together):
+                    words = keep.tile([P, 2 * N_TILE], U8, align_bytes=64, name="w_words%d_%d" % (n, g))
+                    nc.sync.dma_start(out=words[:].bitcast(I32), in_=words_by_partition[:, g, word_cols])
+                    w_words[n].append(words)
+                    w_planes[n].append(planes[:, g - first_pass, :])
 
-        load_x(0)
-        load_x(1)
-        load_x(2)
-        load_w(0)
-        load_x(3)
-        load_w(1)
-        load_w(2)
-        load_w(3)
+        for j in range(TOKEN_TILES):
+            load_x(j)
+        for n in range(FEATURE_TILES):
+            load_w(n)
 
         x_codes = []
         x_planes = []
@@ -114,7 +119,7 @@ def tile_combcrossattention_pa_kernel(tc, hidden_states, Wq_words, Wq_scales, q_
                             bank[:, gg, u, :], x_words[:, first + u : first + WORDS_PER_PASS : 2], identity[:]
                         )
                 grouped = keep.tile([P, 2 * P * 4], BF16, align_bytes=64, name="grouped%d_%d" % (j, half))
-                copy_out = nc.scalar.copy if j == LATE_TILE or half == 1 else nc.vector.tensor_copy
+                copy_out = nc.scalar.copy if half == 1 else nc.vector.tensor_copy
                 copy_out(
                     out=grouped[:].bitcast(F32).rearrange("p (g r u) -> p g r u", g=2, u=2),
                     in_=bank[:].rearrange("p g u r -> p g r u"),
@@ -125,7 +130,7 @@ def tile_combcrossattention_pa_kernel(tc, hidden_states, Wq_words, Wq_scales, q_
                 x_codes[j].append(codes)
                 x_planes[j].append(planes)
 
-        for j in range(LATE_TILE):
+        for j in range(TOKEN_TILES):
             prepare_x(j)
 
         gain_bank = psum.tile([P, BANK], F32, tag="bank")
@@ -133,24 +138,24 @@ def tile_combcrossattention_pa_kernel(tc, hidden_states, Wq_words, Wq_scales, q_
         gain = const.tile([P, HEAD_DIM], F32)
         nc.vector.tensor_copy(out=gain[:], in_=gain_bank[:, 0:HEAD_DIM])
 
-        def project(n, j, first_head, head_count):
-            width = head_count * HEAD_DIM
-            first = first_head * HEAD_DIM
-            q_bank = psum.tile([P, width], F32, tag="bank")
+        def project(n, token_tiles):
+            q_banks = []
+            for j in token_tiles:
+                q_bank = psum.tile([P, N_TILE], F32, tag="bank")
+                q_banks.append(q_bank)
             for g in range(PASSES):
                 tokens = slice((g % 2) * P, (g % 2 + 1) * P)
-                nc.tensor.matmul_mx(
-                    out=q_bank[:],
-                    lhsT=x_codes[j][g // 2][:, tokens].bitcast(FP8X4),
-                    lhsT_scale=x_planes[j][g // 2][:, tokens],
-                    rhs=w_words[n][g // PASSES_PER_LOAD][
-                        :, g % PASSES_PER_LOAD, 2 * first : 2 * (first + width)
-                    ].bitcast(FP4X4),
-                    rhs_scale=w_planes[n][:, g, first : first + width],
-                    start=(g == 0),
-                    stop=(g == PASSES - 1),
-                )
-            return q_bank
+                for j, q_bank in zip(token_tiles, q_banks):
+                    nc.tensor.matmul_mx(
+                        out=q_bank[:],
+                        lhsT=x_codes[j][g // 2][:, tokens].bitcast(FP8X4),
+                        lhsT_scale=x_planes[j][g // 2][:, tokens],
+                        rhs=w_words[n][g][:].bitcast(FP4X4),
+                        rhs_scale=w_planes[n][g],
+                        start=(g == 0),
+                        stop=(g == PASSES - 1),
+                    )
+            return q_banks
 
         def normalise(n, j, first_head, head_count, q_bank, normed):
             sum_sq = stats.tile([P, HEADS_PER_TILE], F32)
@@ -186,12 +191,9 @@ def tile_combcrossattention_pa_kernel(tc, hidden_states, Wq_words, Wq_scales, q_
                 elif j == TOKEN_TILES - 1:
                     nc.sync.dma_start(out=head_rows, in_=normed[:, hh, :, :])
 
-        def whole_bank(n, j, normed):
-            normalise(n, j, 0, HEADS_PER_TILE, project(n, j, 0, HEADS_PER_TILE), normed)
-
         for n in range(FEATURE_TILES):
             normed = results.tile([P, HEADS_PER_TILE, TOKEN_TILES, HEAD_DIM], F32)
-            for j in range(TOKEN_TILES):
-                if n == 0 and j == 1:
-                    prepare_x(LATE_TILE)
-                whole_bank(n, j, normed)
+            groups = [[0, 1, 2], [3]] if n == 0 else [[j] for j in range(TOKEN_TILES)]
+            for token_tiles in groups:
+                for j, q_bank in zip(token_tiles, project(n, token_tiles)):
+                    normalise(n, j, 0, HEADS_PER_TILE, q_bank, normed)

@@ -27,6 +27,7 @@ FEATURE_TILES = HEADS * HEAD_DIM // N_TILE
 HEADS_PER_TILE = N_TILE // HEAD_DIM
 WORDS_PER_PASS = K_PASS // 2
 PASSES_TOGETHER = [2, 4, 4, 4]
+FIRST_TILE_STORED_BY_BANK = 2
 K_HALF = K // 2
 
 FLOPS = 2 * TOKENS * K * HEADS * HEAD_DIM
@@ -186,10 +187,15 @@ def tile_combcrossattention_pa_kernel(tc, hidden_states, Wq_words, Wq_scales, q_
                     op1=MULT,
                 )
                 head_rows = out[n * HEADS_PER_TILE + hh].rearrange("(p j) d -> p j d", j=TOKEN_TILES)
-                if n == FEATURE_TILES - 1:
+                if n == FEATURE_TILES - 1 and j == TOKEN_TILES - 1:
                     nc.sync.dma_start(out=head_rows[:, j, :], in_=normed[:, hh, j, :])
-                elif j == TOKEN_TILES - 1:
+                elif n < FIRST_TILE_STORED_BY_BANK and j == TOKEN_TILES - 1:
                     nc.sync.dma_start(out=head_rows, in_=normed[:, hh, :, :])
+            if n >= FIRST_TILE_STORED_BY_BANK and not (n == FEATURE_TILES - 1 and j == TOKEN_TILES - 1):
+                bank_rows = out[n * HEADS_PER_TILE : (n + 1) * HEADS_PER_TILE].rearrange(
+                    "h (p j) d -> p j h d", j=TOKEN_TILES
+                )
+                nc.sync.dma_start(out=bank_rows[:, j], in_=normed[:, :, j, :])
 
         for n in range(FEATURE_TILES):
             normed = results.tile([P, HEADS_PER_TILE, TOKEN_TILES, HEAD_DIM], F32)

@@ -26,7 +26,6 @@ N_TILE = BANK
 FEATURE_TILES = HEADS * HEAD_DIM // N_TILE
 HEADS_PER_TILE = N_TILE // HEAD_DIM
 WORDS_PER_PASS = K_PASS // 2
-PASSES_TOGETHER = [2, 4, 4, 4]
 FIRST_TILE_STORED_BY_BANK = 2
 K_HALF = K // 2
 
@@ -49,18 +48,13 @@ def tile_combcrossattention_pa_kernel(tc, hidden_states, Wq_words, Wq_scales, q_
         nc.vector.memset(ones[:], 1.0)
         gain_rows = const.tile([P, HEAD_DIM], BF16)
         nc.vector.memset(gain_rows[:], 0.0)
-        nc.scalar.dma_start(out=gain_rows[0:1, :], in_=q_norm_w.rearrange("(o d) -> o d", o=1))
+        nc.gpsimd.dma_start(out=gain_rows[0:1, :], in_=q_norm_w.rearrange("(o d) -> o d", o=1))
         eps = const.tile([P, 1], F32)
         nc.vector.memset(eps[:], EPS)
-        plane_tiles = []
-        for n in range(FEATURE_TILES):
-            plane_tiles.append([])
-            for first_pass in range(0, PASSES, PASSES_TOGETHER[n]):
-                planes = keep.tile(
-                    [P, PASSES_TOGETHER[n], N_TILE], U8, align_bytes=64, name="w_planes%d_%d" % (n, first_pass)
-                )
-                nc.vector.memset(planes[:].bitcast(I32), 0)
-                plane_tiles[n].append(planes)
+        first_planes = keep.tile([P, PASSES, N_TILE], U8, align_bytes=64)
+        nc.vector.memset(first_planes[:].bitcast(I32), 0)
+        later_planes = keep.tile([P, PASSES, (FEATURE_TILES - 1) * N_TILE], U8, align_bytes=64)
+        nc.vector.memset(later_planes[:].bitcast(I32), 0)
         table_warmer = const.tile([P, 1], F32)
         nc.scalar.activation(out=table_warmer[:], in_=eps[:], func=INV_SQRT)
 
@@ -68,40 +62,32 @@ def tile_combcrossattention_pa_kernel(tc, hidden_states, Wq_words, Wq_scales, q_
         x_by_tile = hidden_states.rearrange("(p j) k -> j p k", j=TOKEN_TILES)
 
         def load_x(j):
-            x_rows.append([])
-            for half in range(2):
-                rows = keep.tile([P, K_HALF], BF16, name="x_rows%d_%d" % (j, half))
-                nc.sync.dma_start(out=rows[:], in_=x_by_tile[j][:, half * K_HALF : (half + 1) * K_HALF])
-                x_rows[j].append(rows)
+            rows = keep.tile([P, K], BF16, name="x_rows%d" % j)
+            nc.sync.dma_start(out=rows[:], in_=x_by_tile[j])
+            x_rows.append([rows[:, half * K_HALF : (half + 1) * K_HALF] for half in range(2)])
 
         w_words = []
         scale_rows = Wq_scales.bitcast(I32).rearrange("g q c -> q g c")
         words_by_partition = Wq_words.bitcast(I32).rearrange("g p c -> p g c")
 
-        w_planes = []
 
         def load_w(n):
-            scale_cols = slice(n * N_TILE // 4, (n + 1) * N_TILE // 4)
             word_cols = slice(n * N_TILE // 2, (n + 1) * N_TILE // 2)
             w_words.append([])
-            w_planes.append([])
-            together = PASSES_TOGETHER[n]
-            for first_pass in range(0, PASSES, together):
-                planes = plane_tiles[n][first_pass // together]
-                for r in range(4):
-                    nc.sync.dma_start(
-                        out=planes[r:P:32].bitcast(I32),
-                        in_=scale_rows[r:16:4, first_pass : first_pass + together, scale_cols],
-                    )
-                for g in range(first_pass, first_pass + together):
-                    words = keep.tile([P, 2 * N_TILE], U8, align_bytes=64, name="w_words%d_%d" % (n, g))
-                    nc.sync.dma_start(out=words[:].bitcast(I32), in_=words_by_partition[:, g, word_cols])
-                    w_words[n].append(words)
-                    w_planes[n].append(planes[:, g - first_pass, :])
+            for g in range(PASSES):
+                words = keep.tile([P, 2 * N_TILE], U8, align_bytes=64, name="w_words%d_%d" % (n, g))
+                nc.sync.dma_start(out=words[:].bitcast(I32), in_=words_by_partition[:, g, word_cols])
+                w_words[n].append(words)
 
         for j in range(TOKEN_TILES):
             load_x(j)
-        for n in range(FEATURE_TILES):
+        first_cols = N_TILE // 4
+        for r in range(4):
+            nc.sync.dma_start(out=first_planes[r:P:32].bitcast(I32), in_=scale_rows[r:16:4, :, 0:first_cols])
+        load_w(0)
+        for r in range(4):
+            nc.sync.dma_start(out=later_planes[r:P:32].bitcast(I32), in_=scale_rows[r:16:4, :, first_cols:])
+        for n in range(1, FEATURE_TILES):
             load_w(n)
 
         x_codes = []
@@ -111,7 +97,7 @@ def tile_combcrossattention_pa_kernel(tc, hidden_states, Wq_words, Wq_scales, q_
             x_codes.append([])
             x_planes.append([])
             for half in range(2):
-                x_words = x_rows[j][half][:].bitcast(F32)
+                x_words = x_rows[j][half].bitcast(F32)
                 bank = psum.tile([P, 2, 2, P], F32, tag="bank")
                 for gg in range(2):
                     first = gg * WORDS_PER_PASS
@@ -152,7 +138,9 @@ def tile_combcrossattention_pa_kernel(tc, hidden_states, Wq_words, Wq_scales, q_
                         lhsT=x_codes[j][g // 2][:, tokens].bitcast(FP8X4),
                         lhsT_scale=x_planes[j][g // 2][:, tokens],
                         rhs=w_words[n][g][:].bitcast(FP4X4),
-                        rhs_scale=w_planes[n][g],
+                        rhs_scale=(
+                            first_planes[:, g, :] if n == 0 else later_planes[:, g, (n - 1) * N_TILE : n * N_TILE]
+                        ),
                         start=(g == 0),
                         stop=(g == PASSES - 1),
                     )

@@ -26,6 +26,7 @@ N_TILE = BANK
 FEATURE_TILES = HEADS * HEAD_DIM // N_TILE
 HEADS_PER_TILE = N_TILE // HEAD_DIM
 WORDS_PER_PASS = K_PASS // 2
+BANKS_BY_HEAD = 2
 FIRST_TILE_STORED_BY_BANK = 2
 K_HALF = K // 2
 
@@ -185,9 +186,57 @@ def tile_combcrossattention_pa_kernel(tc, hidden_states, Wq_words, Wq_scales, q_
                 )
                 nc.sync.dma_start(out=bank_rows[:, j], in_=normed[:, :, j, :])
 
-        for n in range(FEATURE_TILES):
+        for n in range(FEATURE_TILES - 1):
             normed = results.tile([P, HEADS_PER_TILE, TOKEN_TILES, HEAD_DIM], F32)
             groups = [[0, 1, 2], [3]] if n == 0 else [[j] for j in range(TOKEN_TILES)]
             for token_tiles in groups:
                 for j, q_bank in zip(token_tiles, project(n, token_tiles)):
                     normalise(n, j, 0, HEADS_PER_TILE, q_bank, normed)
+
+        def project_head(n, j, hh):
+            q_head = psum.tile([P, HEAD_DIM], F32, tag="bank")
+            first = hh * HEAD_DIM
+            for g in range(PASSES):
+                tokens = slice((g % 2) * P, (g % 2 + 1) * P)
+                nc.tensor.matmul_mx(
+                    out=q_head[:],
+                    lhsT=x_codes[j][g // 2][:, tokens].bitcast(FP8X4),
+                    lhsT_scale=x_planes[j][g // 2][:, tokens],
+                    rhs=w_words[n][g][:, 2 * first : 2 * (first + HEAD_DIM)].bitcast(FP4X4),
+                    rhs_scale=later_planes[:, g, (n - 1) * N_TILE + first : (n - 1) * N_TILE + first + HEAD_DIM],
+                    start=(g == 0),
+                    stop=(g == PASSES - 1),
+                )
+            return q_head
+
+        def scale_head(n, j, hh, q_head, sum_sq):
+            inv_rms = stats.tile([P, 1], F32)
+            nc.scalar.activation(out=inv_rms[:], in_=sum_sq[:], func=INV_SQRT, scale=1.0 / HEAD_DIM, bias=eps[:])
+            nc.vector.scalar_tensor_tensor(
+                out=normed[:, hh, j, :], in0=q_head[:], scalar=inv_rms[:], in1=gain[:], op0=MULT, op1=MULT
+            )
+            if j == TOKEN_TILES - 1:
+                head_rows = out[n * HEADS_PER_TILE + hh].rearrange("(p j) d -> p j d", j=TOKEN_TILES)
+                nc.sync.dma_start(out=head_rows[:, j, :], in_=normed[:, hh, j, :])
+            elif hh == HEADS_PER_TILE - 1:
+                bank_rows = out[n * HEADS_PER_TILE : (n + 1) * HEADS_PER_TILE].rearrange(
+                    "h (p j) d -> p j h d", j=TOKEN_TILES
+                )
+                nc.sync.dma_start(out=bank_rows[:, j], in_=normed[:, :, j, :])
+
+        with tc.manual_schedule(engines={mybir.EngineType.PE, mybir.EngineType.Activation}):
+            n = FEATURE_TILES - 1
+            normed = results.tile([P, HEADS_PER_TILE, TOKEN_TILES, HEAD_DIM], F32)
+            for j in range(TOKEN_TILES - BANKS_BY_HEAD):
+                normalise(n, j, 0, HEADS_PER_TILE, project(n, [j])[0], normed)
+            previous = None
+            for j in range(TOKEN_TILES - BANKS_BY_HEAD, TOKEN_TILES):
+                for hh in range(HEADS_PER_TILE):
+                    q_head = project_head(n, j, hh)
+                    sum_sq = stats.tile([P, 1], F32)
+                    squares = stats.tile([P, HEAD_DIM], BF16)
+                    nc.scalar.activation(out=squares[:], in_=q_head[:], func=SQUARE, accum_out=sum_sq[:])
+                    if previous is not None:
+                        scale_head(*previous)
+                    previous = (n, j, hh, q_head, sum_sq)
+            scale_head(*previous)

@@ -107,7 +107,7 @@ def tile_combcrossattention_pa_kernel(tc, hidden_states, Wq_words, Wq_scales, q_
                             bank[:, gg, u, :], x_words[:, first + u : first + WORDS_PER_PASS : 2], identity[:]
                         )
                 grouped = keep.tile([P, 2 * P * 4], BF16, align_bytes=64, name="grouped%d_%d" % (j, half))
-                copy_out = nc.scalar.copy if half == 1 else nc.vector.tensor_copy
+                copy_out = nc.vector.tensor_copy if j == TOKEN_TILES - 1 and half == 0 else nc.scalar.copy
                 copy_out(
                     out=grouped[:].bitcast(F32).rearrange("p (g r u) -> p g r u", g=2, u=2),
                     in_=bank[:].rearrange("p g u r -> p g r u"),

@@ -45,6 +45,8 @@ def tile_combcrossattention_pa_kernel(tc, hidden_states, Wq_words, Wq_scales, q_
 
         identity = const.tile([P, P], F32)
         make_identity(nc, identity[:])
+        first_planes = keep.tile([P, PASSES, N_TILE], U8, align_bytes=64)
+        nc.vector.memset(first_planes[:].bitcast(I32), 0)
         ones = const.tile([P, P], BF16)
         nc.vector.memset(ones[:], 1.0)
         gain_rows = const.tile([P, HEAD_DIM], BF16)
@@ -52,8 +54,6 @@ def tile_combcrossattention_pa_kernel(tc, hidden_states, Wq_words, Wq_scales, q_
         nc.gpsimd.dma_start(out=gain_rows[0:1, :], in_=q_norm_w.rearrange("(o d) -> o d", o=1))
         eps = const.tile([P, 1], F32)
         nc.vector.memset(eps[:], EPS)
-        first_planes = keep.tile([P, PASSES, N_TILE], U8, align_bytes=64)
-        nc.vector.memset(first_planes[:].bitcast(I32), 0)
         later_planes = keep.tile([P, PASSES, (FEATURE_TILES - 1) * N_TILE], U8, align_bytes=64)
         nc.vector.memset(later_planes[:].bitcast(I32), 0)
         table_warmer = const.tile([P, 1], F32)
@@ -80,11 +80,12 @@ def tile_combcrossattention_pa_kernel(tc, hidden_states, Wq_words, Wq_scales, q_
                 nc.sync.dma_start(out=words[:].bitcast(I32), in_=words_by_partition[:, g, word_cols])
                 w_words[n].append(words)
 
-        for j in range(TOKEN_TILES):
-            load_x(j)
         first_cols = N_TILE // 4
+        load_x(0)
         for r in range(4):
             nc.sync.dma_start(out=first_planes[r:P:32].bitcast(I32), in_=scale_rows[r:16:4, :, 0:first_cols])
+        for j in range(1, TOKEN_TILES):
+            load_x(j)
         load_w(0)
         for r in range(4):
             nc.sync.dma_start(out=later_planes[r:P:32].bitcast(I32), in_=scale_rows[r:16:4, :, first_cols:])

from contextlib import ExitStack

import concourse.mybir as mybir
from concourse.masks import make_identity

F32 = mybir.dt.float32
BF16 = mybir.dt.bfloat16
I32 = mybir.dt.int32
U32 = mybir.dt.uint32
U8 = mybir.dt.uint8
FP8X4 = mybir.dt.float8_e4m3fn_x4
FP4X4 = mybir.dt.float4_e2m1fn_x4
MULT = mybir.AluOpType.mult
SQUARE = mybir.ActivationFunctionType.Square
INV_SQRT = mybir.ActivationFunctionType.Abs_reciprocal_sqrt

TOKENS, K, HEADS, HEAD_DIM = 512, 2048, 16, 128
EPS = 1e-5

P = 128
K_PASS = 4 * P
PASSES = K // K_PASS
TOKEN_TILES = TOKENS // P
BANK = 512
N_TILE = BANK
FEATURE_TILES = HEADS * HEAD_DIM // N_TILE
HEADS_PER_TILE = N_TILE // HEAD_DIM
WORDS_PER_PASS = K_PASS // 2
BANKS_BY_HEAD = 2
FIRST_TILE_STORED_BY_BANK = 2
K_HALF = K // 2

FLOPS = 2 * TOKENS * K * HEADS * HEAD_DIM


def tile_combcrossattention_pa_kernel(tc, hidden_states, Wq_words, Wq_scales, q_norm_w, out):
    nc = tc.nc
    with ExitStack() as ctx:
        const = ctx.enter_context(tc.tile_pool(name="const", bufs=1))
        keep = ctx.enter_context(tc.tile_pool(name="keep", bufs=1))
        stats = ctx.enter_context(tc.tile_pool(name="stats", bufs=4))
        results = ctx.enter_context(tc.tile_pool(name="results", bufs=FEATURE_TILES))
        psum = ctx.enter_context(tc.psum_pool(name="psum", bufs=8))
        ctx.enter_context(tc.manual_schedule(engines={mybir.EngineType.PE}))

        identity = const.tile([P, P], F32)
        make_identity(nc, identity[:])
        first_planes = keep.tile([P, PASSES, N_TILE], U8, align_bytes=64)
        nc.vector.memset(first_planes[:].bitcast(I32), 0)
        ones = const.tile([P, P], BF16)
        nc.vector.memset(ones[:], 1.0)
        gain_rows = const.tile([P, HEAD_DIM], BF16)
        nc.vector.memset(gain_rows[:], 0.0)
        nc.gpsimd.dma_start(out=gain_rows[0:1, :], in_=q_norm_w.rearrange("(o d) -> o d", o=1))
        eps = const.tile([P, 1], F32)
        nc.vector.memset(eps[:], EPS)
        later_planes = keep.tile([P, PASSES, (FEATURE_TILES - 1) * N_TILE], U8, align_bytes=64)
        nc.vector.memset(later_planes[:].bitcast(I32), 0)
        table_warmer = const.tile([P, 1], F32)
        nc.scalar.activation(out=table_warmer[:], in_=eps[:], func=INV_SQRT)

        x_rows = []
        x_by_tile = hidden_states.rearrange("(p j) k -> j p k", j=TOKEN_TILES)

        def load_x(j):
            rows = keep.tile([P, K], BF16, name="x_rows%d" % j)
            nc.sync.dma_start(out=rows[:], in_=x_by_tile[j])
            x_rows.append([rows[:, half * K_HALF : (half + 1) * K_HALF] for half in range(2)])

        w_words = []
        scale_rows = Wq_scales.bitcast(I32).rearrange("g q c -> q g c")
        words_by_partition = Wq_words.bitcast(I32).rearrange("g p c -> p g c")


        def load_w(n):
            word_cols = slice(n * N_TILE // 2, (n + 1) * N_TILE // 2)
            w_words.append([])
            for g in range(PASSES):
                words = keep.tile([P, 2 * N_TILE], U8, align_bytes=64, name="w_words%d_%d" % (n, g))
                nc.sync.dma_start(out=words[:].bitcast(I32), in_=words_by_partition[:, g, word_cols])
                w_words[n].append(words)

        first_cols = N_TILE // 4
        load_x(0)
        for r in range(4):
            nc.sync.dma_start(out=first_planes[r:P:32].bitcast(I32), in_=scale_rows[r:16:4, :, 0:first_cols])
        for j in range(1, TOKEN_TILES):
            load_x(j)
        load_w(0)
        for r in range(4):
            nc.sync.dma_start(out=later_planes[r:P:32].bitcast(I32), in_=scale_rows[r:16:4, :, first_cols:])
        for n in range(1, FEATURE_TILES):
            load_w(n)

        x_codes = []
        x_planes = []

        def prepare_x(j):
            x_codes.append([])
            x_planes.append([])
            for half in range(2):
                x_words = x_rows[j][half].bitcast(F32)
                bank = psum.tile([P, 2, 2, P], F32, tag="bank")
                for gg in range(2):
                    first = gg * WORDS_PER_PASS
                    for u in range(2):
                        nc.tensor.transpose(
                            bank[:, gg, u, :], x_words[:, first + u : first + WORDS_PER_PASS : 2], identity[:]
                        )
                grouped = keep.tile([P, 2 * P * 4], BF16, align_bytes=64, name="grouped%d_%d" % (j, half))
                copy_out = nc.vector.tensor_copy if j == TOKEN_TILES - 1 and half == 0 else nc.scalar.copy
                copy_out(
                    out=grouped[:].bitcast(F32).rearrange("p (g r u) -> p g r u", g=2, u=2),
                    in_=bank[:].rearrange("p g u r -> p g r u"),
                )
                codes = keep.tile([P, 2 * P], U32, align_bytes=64, name="x_codes%d_%d" % (j, half))
                planes = keep.tile([P, 2 * P], U8, align_bytes=64, name="x_planes%d_%d" % (j, half))
                nc.vector.quantize_mx(out=codes[:].bitcast(FP8X4), scales=planes[:], in_=grouped[:])
                x_codes[j].append(codes)
                x_planes[j].append(planes)

        for j in range(TOKEN_TILES):
            prepare_x(j)

        gain_bank = psum.tile([P, BANK], F32, tag="bank")
        nc.tensor.matmul(out=gain_bank[:, 0:HEAD_DIM], lhsT=ones[:], rhs=gain_rows[:], start=True, stop=True)
        gain = const.tile([P, HEAD_DIM], F32)
        nc.vector.tensor_copy(out=gain[:], in_=gain_bank[:, 0:HEAD_DIM])

        def project(n, token_tiles):
            q_banks = []
            for j in token_tiles:
                q_bank = psum.tile([P, N_TILE], F32, tag="bank")
                q_banks.append(q_bank)
            for g in range(PASSES):
                tokens = slice((g % 2) * P, (g % 2 + 1) * P)
                for j, q_bank in zip(token_tiles, q_banks):
                    nc.tensor.matmul_mx(
                        out=q_bank[:],
                        lhsT=x_codes[j][g // 2][:, tokens].bitcast(FP8X4),
                        lhsT_scale=x_planes[j][g // 2][:, tokens],
                        rhs=w_words[n][g][:].bitcast(FP4X4),
                        rhs_scale=(
                            first_planes[:, g, :] if n == 0 else later_planes[:, g, (n - 1) * N_TILE : n * N_TILE]
                        ),
                        start=(g == 0),
                        stop=(g == PASSES - 1),
                    )
            return q_banks

        def normalise(n, j, first_head, head_count, q_bank, normed):
            sum_sq = stats.tile([P, HEADS_PER_TILE], F32)
            for i in range(head_count):
                squares = stats.tile([P, HEAD_DIM], BF16)
                nc.scalar.activation(
                    out=squares[:],
                    in_=q_bank[:, i * HEAD_DIM : (i + 1) * HEAD_DIM],
                    func=SQUARE,
                    accum_out=sum_sq[:, i : i + 1],
                )
            inv_rms = stats.tile([P, HEADS_PER_TILE], F32)
            nc.scalar.activation(
                out=inv_rms[:, 0:head_count],
                in_=sum_sq[:, 0:head_count],
                func=INV_SQRT,
                scale=1.0 / HEAD_DIM,
                bias=eps[:],
            )
            for i in range(head_count):
                hh = first_head + i
                nc.vector.scalar_tensor_tensor(
                    out=normed[:, hh, j, :],
                    in0=q_bank[:, i * HEAD_DIM : (i + 1) * HEAD_DIM],
                    scalar=inv_rms[:, i : i + 1],
                    in1=gain[:],
                    op0=MULT,
                    op1=MULT,
                )
                head_rows = out[n * HEADS_PER_TILE + hh].rearrange("(p j) d -> p j d", j=TOKEN_TILES)
                if n == FEATURE_TILES - 1 and j == TOKEN_TILES - 1:
                    nc.sync.dma_start(out=head_rows[:, j, :], in_=normed[:, hh, j, :])
                elif n < FIRST_TILE_STORED_BY_BANK and j == TOKEN_TILES - 1:
                    nc.sync.dma_start(out=head_rows, in_=normed[:, hh, :, :])
            if n >= FIRST_TILE_STORED_BY_BANK and not (n == FEATURE_TILES - 1 and j == TOKEN_TILES - 1):
                bank_rows = out[n * HEADS_PER_TILE : (n + 1) * HEADS_PER_TILE].rearrange(
                    "h (p j) d -> p j h d", j=TOKEN_TILES
                )
                nc.sync.dma_start(out=bank_rows[:, j], in_=normed[:, :, j, :])

        for n in range(FEATURE_TILES - 1):
            normed = results.tile([P, HEADS_PER_TILE, TOKEN_TILES, HEAD_DIM], F32)
            groups = [[0, 1, 2], [3]] if n == 0 else [[j] for j in range(TOKEN_TILES)]
            for token_tiles in groups:
                for j, q_bank in zip(token_tiles, project(n, token_tiles)):
                    normalise(n, j, 0, HEADS_PER_TILE, q_bank, normed)

        def project_head(n, j, hh):
            q_head = psum.tile([P, HEAD_DIM], F32, tag="bank")
            first = hh * HEAD_DIM
            for g in range(PASSES):
                tokens = slice((g % 2) * P, (g % 2 + 1) * P)
                nc.tensor.matmul_mx(
                    out=q_head[:],
                    lhsT=x_codes[j][g // 2][:, tokens].bitcast(FP8X4),
                    lhsT_scale=x_planes[j][g // 2][:, tokens],
                    rhs=w_words[n][g][:, 2 * first : 2 * (first + HEAD_DIM)].bitcast(FP4X4),
                    rhs_scale=later_planes[:, g, (n - 1) * N_TILE + first : (n - 1) * N_TILE + first + HEAD_DIM],
                    start=(g == 0),
                    stop=(g == PASSES - 1),
                )
            return q_head

        def scale_head(n, j, hh, q_head, sum_sq):
            inv_rms = stats.tile([P, 1], F32)
            nc.scalar.activation(out=inv_rms[:], in_=sum_sq[:], func=INV_SQRT, scale=1.0 / HEAD_DIM, bias=eps[:])
            nc.vector.scalar_tensor_tensor(
                out=normed[:, hh, j, :], in0=q_head[:], scalar=inv_rms[:], in1=gain[:], op0=MULT, op1=MULT
            )
            if j == TOKEN_TILES - 1:
                head_rows = out[n * HEADS_PER_TILE + hh].rearrange("(p j) d -> p j d", j=TOKEN_TILES)
                nc.sync.dma_start(out=head_rows[:, j, :], in_=normed[:, hh, j, :])
            elif hh == HEADS_PER_TILE - 1:
                bank_rows = out[n * HEADS_PER_TILE : (n + 1) * HEADS_PER_TILE].rearrange(
                    "h (p j) d -> p j h d", j=TOKEN_TILES
                )
                nc.sync.dma_start(out=bank_rows[:, j], in_=normed[:, :, j, :])

        with tc.manual_schedule(engines={mybir.EngineType.PE, mybir.EngineType.Activation}):
            n = FEATURE_TILES - 1
            normed = results.tile([P, HEADS_PER_TILE, TOKEN_TILES, HEAD_DIM], F32)
            for j in range(TOKEN_TILES - BANKS_BY_HEAD):
                normalise(n, j, 0, HEADS_PER_TILE, project(n, [j])[0], normed)
            previous = None
            for j in range(TOKEN_TILES - BANKS_BY_HEAD, TOKEN_TILES):
                for hh in range(HEADS_PER_TILE):
                    q_head = project_head(n, j, hh)
                    sum_sq = stats.tile([P, 1], F32)
                    squares = stats.tile([P, HEAD_DIM], BF16)
                    nc.scalar.activation(out=squares[:], in_=q_head[:], func=SQUARE, accum_out=sum_sq[:])
                    if previous is not None:
                        scale_head(*previous)
                    previous = (n, j, hh, q_head, sum_sq)
            scale_head(*previous)
